import numpy as np
import ml_dtypes

BF16 = ml_dtypes.bfloat16


def bf(x):
    return np.asarray(x, np.float32).astype(BF16)


def f32(x):
    return np.asarray(x, np.float32)


def f64(x):
    return np.asarray(x).astype(np.float64)


def striped(idx):
    return np.tile(idx.reshape(-1, 16).T, (8, 1))


S, D, M, N = 256, 128, 256, 128


def setup_inputs():
    return {"table": bf(np.random.standard_normal((D, S))), "w": bf(np.random.standard_normal((D, M)) / np.sqrt(D)), "pos": f32(0.5 * np.random.standard_normal((D, N))), "point": f32(np.random.standard_normal((D, 1))), "b": f32(0.1 * np.random.standard_normal((M, 1))), "offs": striped(np.random.permutation(np.tile(np.arange(S), 2))[:N])}


def reference(table, w, pos, point, b, offs):
    idx = offs[:16].T.reshape(-1)
    cond = f64(pos) + f64(point)
    return f64(w).T @ f64(table)[:, idx] + f64(w).T @ cond + f64(b)

@@ -1,0 +1,54 @@
+import concourse.mybir as mybir
+
+BF16, F32, U16 = mybir.dt.bfloat16, mybir.dt.float32, mybir.dt.uint16
+ADD = mybir.AluOpType.add
+
+P = 128
+S = 256
+M = 256
+N = 128
+BLOCKS = M // P
+
+FLOPS = 2 * (2 * P * M * N)
+
+
+def tile_trajectorydecoder_kernel(tc, table, w, pos, point, b, offs, out):
+    nc = tc.nc
+    with (
+        tc.tile_pool(name="held", bufs=1) as held,
+        tc.psum_pool(name="psum", bufs=1) as psum,
+    ):
+        pos_sb = held.tile([P, N], F32, name="pos_sb")
+        nc.sync.dma_start(pos_sb[:], pos)
+        point_sb = held.tile([P, 1], F32, name="point_sb")
+        nc.scalar.dma_start(point_sb[:], point)
+        offsets = held.tile([P, N // 16], U16, name="offsets")
+        nc.sync.dma_start(offsets[:], offs)
+        w_sb = held.tile([P, M], BF16, name="w_sb")
+        nc.scalar.dma_start(w_sb[:], w)
+        table_sb = held.tile([P, S], BF16, name="table_sb")
+        nc.sync.dma_start(table_sb[:], table)
+        bias_sb = held.tile([P, BLOCKS], F32, name="bias_sb")
+        with nc.allow_non_contiguous_dma(reason="256 biases, one to a partition and block"):
+            nc.scalar.dma_start(bias_sb[:], b.rearrange("(t p) o -> p (t o)", p=P))
+
+        cond = held.tile([P, N], BF16, name="cond")
+        nc.vector.tensor_scalar(cond[:], pos_sb[:], point_sb[:, 0:1], None, ADD)
+
+        sums = [psum.tile([P, N], F32, name=f"sum{t}") for t in range(BLOCKS)]
+        for t in range(BLOCKS):
+            nc.tensor.matmul(
+                sums[t][:],
+                w_sb[:, t * P : (t + 1) * P],
+                table_sb[:].indirect(offsets[:]),
+                start=True,
+                stop=False,
+            )
+        for t in range(BLOCKS):
+            nc.tensor.matmul(sums[t][:], w_sb[:, t * P : (t + 1) * P], cond[:], start=False, stop=True)
+
+        store_queues = (nc.sync, nc.scalar)
+        for t in range(BLOCKS):
+            logits = held.tile([P, N], F32, name=f"logits{t}")
+            nc.vector.tensor_scalar(logits[:], sums[t][:], bias_sb[:, t : t + 1], None, ADD)
+            store_queues[t].dma_start(out[t * P : (t + 1) * P, :], logits[:])

@@ -8,6 +8,8 @@ S = 256
 M = 256
 N = 128
 BLOCKS = M // P
+WARM_COLS = 512
+WARM_MATMULS = 4
 
 FLOPS = 2 * (2 * P * M * N)
 
@@ -31,6 +33,12 @@ def tile_trajectorydecoder_kernel(tc, table, w, pos, point, b, offs, out):
         bias_sb = held.tile([P, BLOCKS], F32, name="bias_sb")
         with nc.allow_non_contiguous_dma(reason="256 biases, one to a partition and block"):
             nc.scalar.dma_start(bias_sb[:], b.rearrange("(t p) o -> p (t o)", p=P))
+
+        zeros = held.tile([P, WARM_COLS], BF16, name="zeros")
+        nc.vector.memset(zeros[:], 0.0)
+        unused = psum.tile([P, WARM_COLS], F32, name="unused")
+        for turn in range(WARM_MATMULS):
+            nc.tensor.matmul(unused[:], zeros[:, 0:P], zeros[:], start=True, stop=True)
 
         cond = held.tile([P, N], BF16, name="cond")
         nc.vector.tensor_scalar(cond[:], pos_sb[:], point_sb[:, 0:1], None, ADD)

@@ -1,4 +1,5 @@
 import concourse.mybir as mybir
+from concourse.masks import make_identity
 
 BF16, F32, U16 = mybir.dt.bfloat16, mybir.dt.float32, mybir.dt.uint16
 ADD = mybir.AluOpType.add
@@ -8,8 +9,7 @@ S = 256
 M = 256
 N = 128
 BLOCKS = M // P
-WARM_COLS = 512
-WARM_MATMULS = 4
+ROWS = 1 + BLOCKS
 
 FLOPS = 2 * (2 * P * M * N)
 
@@ -22,26 +22,25 @@ def tile_trajectorydecoder_kernel(tc, table, w, pos, point, b, offs, out):
     ):
         pos_sb = held.tile([P, N], F32, name="pos_sb")
         nc.sync.dma_start(pos_sb[:], pos)
-        point_sb = held.tile([P, 1], F32, name="point_sb")
-        nc.scalar.dma_start(point_sb[:], point)
+        rows = held.tile([ROWS, P], F32, name="rows")
+        nc.scalar.dma_start(rows[0:1, :], point.rearrange("k o -> o k"))
+        nc.scalar.dma_start(rows[1:ROWS, :], b.rearrange("(t p) o -> t (p o)", p=P))
         offsets = held.tile([P, N // 16], U16, name="offsets")
         nc.sync.dma_start(offsets[:], offs)
         w_sb = held.tile([P, M], BF16, name="w_sb")
         nc.scalar.dma_start(w_sb[:], w)
         table_sb = held.tile([P, S], BF16, name="table_sb")
         nc.sync.dma_start(table_sb[:], table)
-        bias_sb = held.tile([P, BLOCKS], F32, name="bias_sb")
-        with nc.allow_non_contiguous_dma(reason="256 biases, one to a partition and block"):
-            nc.scalar.dma_start(bias_sb[:], b.rearrange("(t p) o -> p (t o)", p=P))
 
-        zeros = held.tile([P, WARM_COLS], BF16, name="zeros")
-        nc.vector.memset(zeros[:], 0.0)
-        unused = psum.tile([P, WARM_COLS], F32, name="unused")
-        for turn in range(WARM_MATMULS):
-            nc.tensor.matmul(unused[:], zeros[:, 0:P], zeros[:], start=True, stop=True)
+        identity = held.tile([ROWS, ROWS], F32, name="identity")
+        make_identity(nc, identity[:])
+        columns_ps = psum.tile([P, ROWS], F32, name="columns_ps")
+        nc.tensor.matmul(columns_ps[:], rows[:], identity[:], start=True, stop=True)
+        columns = held.tile([P, ROWS], F32, name="columns")
+        nc.vector.tensor_copy(columns[:], columns_ps[:])
 
         cond = held.tile([P, N], BF16, name="cond")
-        nc.vector.tensor_scalar(cond[:], pos_sb[:], point_sb[:, 0:1], None, ADD)
+        nc.vector.tensor_scalar(cond[:], pos_sb[:], columns[:, 0:1], None, ADD)
 
         sums = [psum.tile([P, N], F32, name=f"sum{t}") for t in range(BLOCKS)]
         for t in range(BLOCKS):
@@ -58,5 +57,5 @@ def tile_trajectorydecoder_kernel(tc, table, w, pos, point, b, offs, out):
         store_queues = (nc.sync, nc.scalar)
         for t in range(BLOCKS):
             logits = held.tile([P, N], F32, name=f"logits{t}")
-            nc.vector.tensor_scalar(logits[:], sums[t][:], bias_sb[:, t : t + 1], None, ADD)
+            nc.vector.tensor_scalar(logits[:], sums[t][:], columns[:, 1 + t : 2 + t], None, ADD)
             store_queues[t].dma_start(out[t * P : (t + 1) * P, :], logits[:])

@@ -1,5 +1,4 @@
 import concourse.mybir as mybir
-from concourse.masks import make_identity
 
 BF16, F32, U16 = mybir.dt.bfloat16, mybir.dt.float32, mybir.dt.uint16
 ADD = mybir.AluOpType.add
@@ -9,7 +8,6 @@ S = 256
 M = 256
 N = 128
 BLOCKS = M // P
-ROWS = 1 + BLOCKS
 
 FLOPS = 2 * (2 * P * M * N)
 
@@ -20,27 +18,22 @@ def tile_trajectorydecoder_kernel(tc, table, w, pos, point, b, offs, out):
         tc.tile_pool(name="held", bufs=1) as held,
         tc.psum_pool(name="psum", bufs=1) as psum,
     ):
-        pos_sb = held.tile([P, N], F32, name="pos_sb")
-        nc.sync.dma_start(pos_sb[:], pos)
-        rows = held.tile([ROWS, P], F32, name="rows")
-        nc.scalar.dma_start(rows[0:1, :], point.rearrange("k o -> o k"))
-        nc.scalar.dma_start(rows[1:ROWS, :], b.rearrange("(t p) o -> t (p o)", p=P))
         offsets = held.tile([P, N // 16], U16, name="offsets")
         nc.sync.dma_start(offsets[:], offs)
         w_sb = held.tile([P, M], BF16, name="w_sb")
         nc.scalar.dma_start(w_sb[:], w)
         table_sb = held.tile([P, S], BF16, name="table_sb")
         nc.sync.dma_start(table_sb[:], table)
-
-        identity = held.tile([ROWS, ROWS], F32, name="identity")
-        make_identity(nc, identity[:])
-        columns_ps = psum.tile([P, ROWS], F32, name="columns_ps")
-        nc.tensor.matmul(columns_ps[:], rows[:], identity[:], start=True, stop=True)
-        columns = held.tile([P, ROWS], F32, name="columns")
-        nc.vector.tensor_copy(columns[:], columns_ps[:])
+        point_sb = held.tile([P, 1], F32, name="point_sb")
+        nc.scalar.dma_start(point_sb[:], point)
+        pos_sb = held.tile([P, N], F32, name="pos_sb")
+        nc.sync.dma_start(pos_sb[:], pos)
+        bias_sb = held.tile([P, BLOCKS], F32, name="bias_sb")
+        with nc.allow_non_contiguous_dma(reason="256 biases, one to a partition and block"):
+            nc.scalar.dma_start(bias_sb[:], b.rearrange("(t p) o -> p (t o)", p=P))
 
         cond = held.tile([P, N], BF16, name="cond")
-        nc.vector.tensor_scalar(cond[:], pos_sb[:], columns[:, 0:1], None, ADD)
+        nc.vector.tensor_scalar(cond[:], pos_sb[:], point_sb[:, 0:1], None, ADD)
 
         sums = [psum.tile([P, N], F32, name=f"sum{t}") for t in range(BLOCKS)]
         for t in range(BLOCKS):
@@ -57,5 +50,5 @@ def tile_trajectorydecoder_kernel(tc, table, w, pos, point, b, offs, out):
         store_queues = (nc.sync, nc.scalar)
         for t in range(BLOCKS):
             logits = held.tile([P, N], F32, name=f"logits{t}")
-            nc.vector.tensor_scalar(logits[:], sums[t][:], columns[:, 1 + t : 2 + t], None, ADD)
+            nc.vector.tensor_scalar(logits[:], sums[t][:], bias_sb[:, t : t + 1], None, ADD)
             store_queues[t].dma_start(out[t * P : (t + 1) * P, :], logits[:])

@@ -18,19 +18,19 @@ def tile_trajectorydecoder_kernel(tc, table, w, pos, point, b, offs, out):
         tc.tile_pool(name="held", bufs=1) as held,
         tc.psum_pool(name="psum", bufs=1) as psum,
     ):
+        bias_sb = held.tile([P, BLOCKS], F32, name="bias_sb")
+        with nc.allow_non_contiguous_dma(reason="256 biases, one to a partition and block"):
+            nc.sync.dma_start(bias_sb[:], b.rearrange("(t p) o -> p (t o)", p=P))
+        point_sb = held.tile([P, 1], F32, name="point_sb")
+        nc.scalar.dma_start(point_sb[:], point)
         offsets = held.tile([P, N // 16], U16, name="offsets")
         nc.sync.dma_start(offsets[:], offs)
         w_sb = held.tile([P, M], BF16, name="w_sb")
         nc.scalar.dma_start(w_sb[:], w)
         table_sb = held.tile([P, S], BF16, name="table_sb")
         nc.sync.dma_start(table_sb[:], table)
-        point_sb = held.tile([P, 1], F32, name="point_sb")
-        nc.scalar.dma_start(point_sb[:], point)
         pos_sb = held.tile([P, N], F32, name="pos_sb")
-        nc.sync.dma_start(pos_sb[:], pos)
-        bias_sb = held.tile([P, BLOCKS], F32, name="bias_sb")
-        with nc.allow_non_contiguous_dma(reason="256 biases, one to a partition and block"):
-            nc.scalar.dma_start(bias_sb[:], b.rearrange("(t p) o -> p (t o)", p=P))
+        nc.scalar.dma_start(pos_sb[:], pos)
 
         cond = held.tile([P, N], BF16, name="cond")
         nc.vector.tensor_scalar(cond[:], pos_sb[:], point_sb[:, 0:1], None, ADD)

@@ -18,19 +18,19 @@ def tile_trajectorydecoder_kernel(tc, table, w, pos, point, b, offs, out):
         tc.tile_pool(name="held", bufs=1) as held,
         tc.psum_pool(name="psum", bufs=1) as psum,
     ):
-        bias_sb = held.tile([P, BLOCKS], F32, name="bias_sb")
-        with nc.allow_non_contiguous_dma(reason="256 biases, one to a partition and block"):
-            nc.sync.dma_start(bias_sb[:], b.rearrange("(t p) o -> p (t o)", p=P))
+        pos_sb = held.tile([P, N], F32, name="pos_sb")
+        nc.scalar.dma_start(pos_sb[:], pos)
         point_sb = held.tile([P, 1], F32, name="point_sb")
-        nc.scalar.dma_start(point_sb[:], point)
+        nc.sync.dma_start(point_sb[:], point)
         offsets = held.tile([P, N // 16], U16, name="offsets")
         nc.sync.dma_start(offsets[:], offs)
         w_sb = held.tile([P, M], BF16, name="w_sb")
         nc.scalar.dma_start(w_sb[:], w)
         table_sb = held.tile([P, S], BF16, name="table_sb")
         nc.sync.dma_start(table_sb[:], table)
-        pos_sb = held.tile([P, N], F32, name="pos_sb")
-        nc.scalar.dma_start(pos_sb[:], pos)
+        bias_sb = held.tile([P, BLOCKS], F32, name="bias_sb")
+        with nc.allow_non_contiguous_dma(reason="256 biases, one to a partition and block"):
+            nc.scalar.dma_start(bias_sb[:], b.rearrange("(t p) o -> p (t o)", p=P))
 
         cond = held.tile([P, N], BF16, name="cond")
         nc.vector.tensor_scalar(cond[:], pos_sb[:], point_sb[:, 0:1], None, ADD)
@@ -47,7 +47,7 @@ def tile_trajectorydecoder_kernel(tc, table, w, pos, point, b, offs, out):
         for t in range(BLOCKS):
             nc.tensor.matmul(sums[t][:], w_sb[:, t * P : (t + 1) * P], cond[:], start=False, stop=True)
 
-        store_queues = (nc.sync, nc.scalar)
+        store_queues = (nc.scalar, nc.sync)
         for t in range(BLOCKS):
             logits = held.tile([P, N], F32, name=f"logits{t}")
             nc.vector.tensor_scalar(logits[:], sums[t][:], bias_sb[:, t : t + 1], None, ADD)

@@ -2,6 +2,7 @@ import concourse.mybir as mybir
 
 BF16, F32, U16 = mybir.dt.bfloat16, mybir.dt.float32, mybir.dt.uint16
 ADD = mybir.AluOpType.add
+IDENTITY = mybir.ActivationFunctionType.Identity
 
 P = 128
 S = 256
@@ -32,6 +33,10 @@ def tile_trajectorydecoder_kernel(tc, table, w, pos, point, b, offs, out):
         with nc.allow_non_contiguous_dma(reason="256 biases, one to a partition and block"):
             nc.scalar.dma_start(bias_sb[:], b.rearrange("(t p) o -> p (t o)", p=P))
 
+        scrap = held.tile([P, 1], F32, name="scrap")
+        nc.vector.memset(scrap[:], 0.0)
+        nc.scalar.activation(scrap[:], scrap[:], IDENTITY)
+
         cond = held.tile([P, N], BF16, name="cond")
         nc.vector.tensor_scalar(cond[:], pos_sb[:], point_sb[:, 0:1], None, ADD)
 
@@ -47,8 +52,9 @@ def tile_trajectorydecoder_kernel(tc, table, w, pos, point, b, offs, out):
         for t in range(BLOCKS):
             nc.tensor.matmul(sums[t][:], w_sb[:, t * P : (t + 1) * P], cond[:], start=False, stop=True)
 
-        store_queues = (nc.scalar, nc.sync)
-        for t in range(BLOCKS):
-            logits = held.tile([P, N], F32, name=f"logits{t}")
-            nc.vector.tensor_scalar(logits[:], sums[t][:], bias_sb[:, t : t + 1], None, ADD)
-            store_queues[t].dma_start(out[t * P : (t + 1) * P, :], logits[:])
+        logits0 = held.tile([P, N], F32, name="logits0")
+        nc.vector.tensor_scalar(logits0[:], sums[0][:], bias_sb[:, 0:1], None, ADD)
+        nc.sync.dma_start(out[0:P, :], logits0[:])
+        logits1 = held.tile([P, N], F32, name="logits1")
+        nc.scalar.activation(logits1[:], sums[1][:], IDENTITY, bias=bias_sb[:, 1:2])
+        nc.scalar.dma_start(out[P : 2 * P, :], logits1[:])

@@ -9,6 +9,8 @@ S = 256
 M = 256
 N = 128
 BLOCKS = M // P
+WARM_COLS = 512
+WARM_MATMULS = 4
 
 FLOPS = 2 * (2 * P * M * N)
 
@@ -36,6 +38,12 @@ def tile_trajectorydecoder_kernel(tc, table, w, pos, point, b, offs, out):
         scrap = held.tile([P, 1], F32, name="scrap")
         nc.vector.memset(scrap[:], 0.0)
         nc.scalar.activation(scrap[:], scrap[:], IDENTITY)
+
+        zeros = held.tile([P, WARM_COLS], BF16, name="zeros")
+        nc.vector.memset(zeros[:], 0.0)
+        unused = psum.tile([P, WARM_COLS], F32, name="unused")
+        for turn in range(WARM_MATMULS):
+            nc.tensor.matmul(unused[:], zeros[:, 0:P], zeros[:], start=True, stop=True)
 
         cond = held.tile([P, N], BF16, name="cond")
         nc.vector.tensor_scalar(cond[:], pos_sb[:], point_sb[:, 0:1], None, ADD)

@@ -35,15 +35,17 @@ def tile_trajectorydecoder_kernel(tc, table, w, pos, point, b, offs, out):
         with nc.allow_non_contiguous_dma(reason="256 biases, one to a partition and block"):
             nc.scalar.dma_start(bias_sb[:], b.rearrange("(t p) o -> p (t o)", p=P))
 
-        scrap = held.tile([P, 1], F32, name="scrap")
-        nc.vector.memset(scrap[:], 0.0)
-        nc.scalar.activation(scrap[:], scrap[:], IDENTITY)
-
-        zeros = held.tile([P, WARM_COLS], BF16, name="zeros")
+        zeros = held.tile([P, P], BF16, name="zeros")
         nc.vector.memset(zeros[:], 0.0)
         unused = psum.tile([P, WARM_COLS], F32, name="unused")
         for turn in range(WARM_MATMULS):
-            nc.tensor.matmul(unused[:], zeros[:, 0:P], zeros[:], start=True, stop=True)
+            nc.tensor.matmul(
+                unused[:], zeros[:], zeros[:, 0:1].to_broadcast([P, WARM_COLS]), start=True, stop=True
+            )
+
+        scrap = held.tile([P, 1], F32, name="scrap")
+        nc.vector.memset(scrap[:], 0.0)
+        nc.scalar.activation(scrap[:], scrap[:], IDENTITY)
 
         cond = held.tile([P, N], BF16, name="cond")
         nc.vector.tensor_scalar(cond[:], pos_sb[:], point_sb[:, 0:1], None, ADD)

@@ -51,16 +51,11 @@ def tile_trajectorydecoder_kernel(tc, table, w, pos, point, b, offs, out):
         nc.vector.tensor_scalar(cond[:], pos_sb[:], point_sb[:, 0:1], None, ADD)
 
         sums = [psum.tile([P, N], F32, name=f"sum{t}") for t in range(BLOCKS)]
-        for t in range(BLOCKS):
-            nc.tensor.matmul(
-                sums[t][:],
-                w_sb[:, t * P : (t + 1) * P],
-                table_sb[:].indirect(offsets[:]),
-                start=True,
-                stop=False,
-            )
-        for t in range(BLOCKS):
-            nc.tensor.matmul(sums[t][:], w_sb[:, t * P : (t + 1) * P], cond[:], start=False, stop=True)
+        looked_up = table_sb[:].indirect(offsets[:])
+        nc.tensor.matmul(sums[0][:], w_sb[:, 0:P], cond[:], start=True, stop=False)
+        nc.tensor.matmul(sums[0][:], w_sb[:, 0:P], looked_up, start=False, stop=True)
+        nc.tensor.matmul(sums[1][:], w_sb[:, P : 2 * P], looked_up, start=True, stop=False)
+        nc.tensor.matmul(sums[1][:], w_sb[:, P : 2 * P], cond[:], start=False, stop=True)
 
         logits0 = held.tile([P, N], F32, name="logits0")
         nc.vector.tensor_scalar(logits0[:], sums[0][:], bias_sb[:, 0:1], None, ADD)

@@ -22,15 +22,15 @@ def tile_trajectorydecoder_kernel(tc, table, w, pos, point, b, offs, out):
         tc.psum_pool(name="psum", bufs=1) as psum,
     ):
         pos_sb = held.tile([P, N], F32, name="pos_sb")
-        nc.scalar.dma_start(pos_sb[:], pos)
+        nc.sync.dma_start(pos_sb[:], pos)
         point_sb = held.tile([P, 1], F32, name="point_sb")
-        nc.sync.dma_start(point_sb[:], point)
+        nc.scalar.dma_start(point_sb[:], point)
+        w_sb = held.tile([P, M], BF16, name="w_sb")
+        nc.sync.dma_start(w_sb[:], w)
+        table_sb = held.tile([P, S], BF16, name="table_sb")
+        nc.scalar.dma_start(table_sb[:], table)
         offsets = held.tile([P, N // 16], U16, name="offsets")
         nc.sync.dma_start(offsets[:], offs)
-        w_sb = held.tile([P, M], BF16, name="w_sb")
-        nc.scalar.dma_start(w_sb[:], w)
-        table_sb = held.tile([P, S], BF16, name="table_sb")
-        nc.sync.dma_start(table_sb[:], table)
         bias_sb = held.tile([P, BLOCKS], F32, name="bias_sb")
         with nc.allow_non_contiguous_dma(reason="256 biases, one to a partition and block"):
             nc.scalar.dma_start(bias_sb[:], b.rearrange("(t p) o -> p (t o)", p=P))

@@ -58,8 +58,8 @@ def tile_trajectorydecoder_kernel(tc, table, w, pos, point, b, offs, out):
         nc.tensor.matmul(sums[1][:], w_sb[:, P : 2 * P], cond[:], start=False, stop=True)
 
         logits0 = held.tile([P, N], F32, name="logits0")
-        nc.vector.tensor_scalar(logits0[:], sums[0][:], bias_sb[:, 0:1], None, ADD)
-        nc.sync.dma_start(out[0:P, :], logits0[:])
+        nc.scalar.activation(logits0[:], sums[0][:], IDENTITY, bias=bias_sb[:, 0:1])
+        nc.scalar.dma_start(out[0:P, :], logits0[:])
         logits1 = held.tile([P, N], F32, name="logits1")
-        nc.scalar.activation(logits1[:], sums[1][:], IDENTITY, bias=bias_sb[:, 1:2])
-        nc.scalar.dma_start(out[P : 2 * P, :], logits1[:])
+        nc.vector.tensor_scalar(logits1[:], sums[1][:], bias_sb[:, 1:2], None, ADD)
+        nc.sync.dma_start(out[P : 2 * P, :], logits1[:])

import concourse.mybir as mybir

BF16, F32, U16 = mybir.dt.bfloat16, mybir.dt.float32, mybir.dt.uint16
ADD = mybir.AluOpType.add
IDENTITY = mybir.ActivationFunctionType.Identity

P = 128
S = 256
M = 256
N = 128
BLOCKS = M // P
WARM_COLS = 512
WARM_MATMULS = 4

FLOPS = 2 * (2 * P * M * N)


def tile_trajectorydecoder_kernel(tc, table, w, pos, point, b, offs, out):
    nc = tc.nc
    with (
        tc.tile_pool(name="held", bufs=1) as held,
        tc.psum_pool(name="psum", bufs=1) as psum,
    ):
        pos_sb = held.tile([P, N], F32, name="pos_sb")
        nc.sync.dma_start(pos_sb[:], pos)
        point_sb = held.tile([P, 1], F32, name="point_sb")
        nc.scalar.dma_start(point_sb[:], point)
        w_sb = held.tile([P, M], BF16, name="w_sb")
        nc.sync.dma_start(w_sb[:], w)
        table_sb = held.tile([P, S], BF16, name="table_sb")
        nc.scalar.dma_start(table_sb[:], table)
        offsets = held.tile([P, N // 16], U16, name="offsets")
        nc.sync.dma_start(offsets[:], offs)
        bias_sb = held.tile([P, BLOCKS], F32, name="bias_sb")
        with nc.allow_non_contiguous_dma(reason="256 biases, one to a partition and block"):
            nc.scalar.dma_start(bias_sb[:], b.rearrange("(t p) o -> p (t o)", p=P))

        zeros = held.tile([P, P], BF16, name="zeros")
        nc.vector.memset(zeros[:], 0.0)
        unused = psum.tile([P, WARM_COLS], F32, name="unused")
        for turn in range(WARM_MATMULS):
            nc.tensor.matmul(
                unused[:], zeros[:], zeros[:, 0:1].to_broadcast([P, WARM_COLS]), start=True, stop=True
            )

        scrap = held.tile([P, 1], F32, name="scrap")
        nc.vector.memset(scrap[:], 0.0)
        nc.scalar.activation(scrap[:], scrap[:], IDENTITY)

        cond = held.tile([P, N], BF16, name="cond")
        nc.vector.tensor_scalar(cond[:], pos_sb[:], point_sb[:, 0:1], None, ADD)

        sums = [psum.tile([P, N], F32, name=f"sum{t}") for t in range(BLOCKS)]
        looked_up = table_sb[:].indirect(offsets[:])
        nc.tensor.matmul(sums[0][:], w_sb[:, 0:P], cond[:], start=True, stop=False)
        nc.tensor.matmul(sums[0][:], w_sb[:, 0:P], looked_up, start=False, stop=True)
        nc.tensor.matmul(sums[1][:], w_sb[:, P : 2 * P], looked_up, start=True, stop=False)
        nc.tensor.matmul(sums[1][:], w_sb[:, P : 2 * P], cond[:], start=False, stop=True)

        logits0 = held.tile([P, N], F32, name="logits0")
        nc.scalar.activation(logits0[:], sums[0][:], IDENTITY, bias=bias_sb[:, 0:1])
        nc.scalar.dma_start(out[0:P, :], logits0[:])
        logits1 = held.tile([P, N], F32, name="logits1")
        nc.vector.tensor_scalar(logits1[:], sums[1][:], bias_sb[:, 1:2], None, ADD)
        nc.sync.dma_start(out[P : 2 * P, :], logits1[:])
